import numpy as np
import ml_dtypes


def mxq(x, axis, fmt="e4m3"):
    dtype, down = {"e4m3": (ml_dtypes.float8_e4m3fn, 7), "e5m2": (ml_dtypes.float8_e5m2, 14)}[fmt]
    v = np.moveaxis(np.asarray(x, np.float32).astype(ml_dtypes.bfloat16).astype(np.float64), axis, -1)
    blocks = v.reshape(v.shape[:-1] + (-1, 32))
    amax = np.abs(blocks).max(-1, keepdims=True)
    byte = np.maximum(np.where(amax > 0, np.frexp(amax)[1] - 1 + 127, 0) - down, 1)
    scale = np.exp2(byte - 127.0)
    codes = (blocks / scale).astype(np.float32).astype(dtype).astype(np.float64)
    return np.moveaxis((codes * scale).reshape(v.shape), -1, axis)


WIDE = False


def mx_kscale(k):
    if not WIDE:
        return np.ones(k)
    levels = np.array([10, -10, 5, -5, 0])
    a = np.random.permutation(np.resize(levels, k // 512 * 4)).reshape(k // 512, 4)
    idx = np.arange(k)
    return np.exp2(a[idx // 512, idx % 128 // 32])


BF16 = ml_dtypes.bfloat16


def bf(x):
    return np.asarray(x, np.float32).astype(BF16)


def f64(x):
    return np.asarray(x).astype(np.float64)


B, T, E, V, NH, C = 2, 2048, 512, 2048, 4, 512
KD = E // NH
SCALING = KD ** -0.5


def rotate_every_two(x):
    x1 = x[..., 0::2]
    x2 = x[..., 1::2]
    return np.stack((-x2, x1), axis=-1).reshape(x.shape)


def theta_shift(x, sin, cos):
    return x * cos + rotate_every_two(x) * sin


def rope_tables():
    half = np.arange(0, KD, 2) / KD
    angle = np.repeat(1.0 / 10000.0 ** half, 2)
    pos = np.arange(T)
    return np.sin(pos[:, None] * angle[None, :]), np.cos(pos[:, None] * angle[None, :])


def setup_inputs():
    s = mx_kscale(E)
    sin, cos = rope_tables()
    return {"hidden_states": bf(np.random.standard_normal((B, T, E)) * s),
            "wq": bf(np.random.standard_normal((E, E)) / np.sqrt(E) / s[None, :]),
            "wk": bf(np.random.standard_normal((E, E)) * 2.0 / np.sqrt(E) / s[None, :]),
            "sin": bf(sin), "cos": bf(cos)}


def reference(hidden_states, wq, wk, sin, cos):
    xq = mxq(f64(hidden_states), 2, "e4m3")
    q = xq @ mxq(f64(wq), 1, "e4m3").T
    k = xq @ mxq(f64(wk), 1, "e4m3").T
    q = q.reshape(B, T, NH, KD).transpose(0, 2, 1, 3)
    k = k.reshape(B, T, NH, KD).transpose(0, 2, 1, 3) * SCALING
    return theta_shift(q, f64(sin), f64(cos)), theta_shift(k, f64(sin), f64(cos))

@@ -1,0 +1,180 @@
+import concourse.mybir as mybir
+from concourse.masks import make_identity
+
+F32 = mybir.dt.float32
+BF16 = mybir.dt.bfloat16
+U32 = mybir.dt.uint32
+U8 = mybir.dt.uint8
+FP8X4 = mybir.dt.float8_e4m3fn_x4
+MULT = mybir.AluOpType.mult
+ADD = mybir.AluOpType.add
+
+P = 128
+BATCH, SEQ, EMBED, HEADS = 2, 2048, 512, 4
+HEAD_DIM = EMBED // HEADS
+K_FACTOR = HEAD_DIM**-0.5
+BLOCKS = 4
+GROUP = BLOCKS * P
+GROUPS_PER_BATCH = SEQ // GROUP
+GROUPS = BATCH * GROUPS_PER_BATCH
+WORDS = EMBED // 2
+BANK = 512
+PACK = 4
+
+FLOPS = 2 * BATCH * SEQ * EMBED * 2 * EMBED
+
+
+def tile_nucleusxmultiscaleretention_pa_t_kernel(
+    tc, hidden_states, wq, wk, sin, cos, out_0, out_1
+):
+    nc = tc.nc
+    with (
+        tc.tile_pool(name="keep", bufs=1) as keep,
+        tc.tile_pool(name="tokens", bufs=GROUPS) as tokens,
+        tc.tile_pool(name="regroup", bufs=3) as regroup,
+        tc.tile_pool(name="quantised", bufs=2) as quantised,
+        tc.tile_pool(name="results", bufs=3) as results,
+        tc.tile_pool(name="products", bufs=2) as products,
+        tc.psum_pool(name="flipped", bufs=2) as flipped,
+        tc.psum_pool(name="sums", bufs=3) as sums,
+    ):
+        identity = keep.tile([P, P], F32)
+        make_identity(nc, identity[:])
+        pair_swap = keep.tile([P, P], F32)
+        identity_pairs = identity[:].rearrange("p (j two) -> p j two", two=2)
+        pair_swap_pairs = pair_swap[:].rearrange("p (j two) -> p j two", two=2)
+        nc.vector.tensor_copy(out=pair_swap_pairs[:, :, 0:1], in_=identity_pairs[:, :, 1:2])
+        nc.vector.tensor_copy(out=pair_swap_pairs[:, :, 1:2], in_=identity_pairs[:, :, 0:1])
+
+        def load_weight(w, tag):
+            rows = keep.tile([P, BLOCKS * EMBED], BF16, name=tag + "_rows")
+            nc.sync.dma_start(
+                out=rows[:].rearrange("p (h k) -> p h k", h=BLOCKS),
+                in_=w.rearrange("(h p) k -> p h k", p=P),
+            )
+            return rows
+
+        def load_tokens(group):
+            b, place = divmod(group, GROUPS_PER_BATCH)
+            rows = tokens.tile([P, BLOCKS * EMBED], BF16, name="token_rows")
+            nc.sync.dma_start(
+                out=rows[:],
+                in_=hidden_states[b, place * GROUP : (place + 1) * GROUP, :].rearrange(
+                    "(p i) k -> p (i k)", i=BLOCKS
+                ),
+            )
+            return rows
+
+        def load_table(table, tag):
+            rows = keep.tile([P, GROUPS_PER_BATCH, BLOCKS, HEAD_DIM], BF16, name=tag)
+            nc.sync.dma_start(
+                out=rows[:].rearrange("p g i d -> p g (i d)"),
+                in_=table.rearrange("(g p i) d -> p g (i d)", p=P, i=BLOCKS),
+            )
+            return rows
+
+        wq_rows = load_weight(wq, "wq")
+        token_rows = [load_tokens(0)]
+        sin_signed = load_table(sin, "sin_signed")
+        cos_table = load_table(cos, "cos_table")
+        wk_rows = load_weight(wk, "wk")
+        for group in range(1, GROUPS):
+            token_rows.append(load_tokens(group))
+
+        def quantise_rows(rows, permutation, codes, scales):
+            words = rows[:].bitcast(F32)
+            grouped = regroup.tile([P, GROUP * PACK], BF16, align_bytes=64)
+            grouped_words = grouped[:].bitcast(F32).rearrange(
+                "p (j r u) -> p j r u", j=BLOCKS, u=2
+            )
+            for first in range(0, BLOCKS, 2):
+                bank = flipped.tile([P, BANK], F32)
+                for j in range(2):
+                    for u in range(2):
+                        nc.tensor.transpose(
+                            bank[:, (2 * j + u) * P : (2 * j + u + 1) * P],
+                            words[:, (first + j) * WORDS + u * P : (first + j) * WORDS + (u + 1) * P],
+                            permutation[:],
+                        )
+                nc.scalar.copy(
+                    out=grouped_words[:, first : first + 2],
+                    in_=bank[:].rearrange("p (j u r) -> p j r u", j=2, u=2),
+                )
+            nc.vector.quantize_mx(out=codes.bitcast(FP8X4), scales=scales, in_=grouped[:])
+
+        def quantise_weight(rows, tag):
+            codes = keep.tile([P, 2, GROUP], U32, name=tag + "_codes", align_bytes=64)
+            scales = keep.tile([P, 2, GROUP], U8, name=tag + "_scales", align_bytes=64)
+            quantise_rows(rows, identity, codes[:, 0, :], scales[:, 0, :])
+            quantise_rows(rows, pair_swap, codes[:, 1, :], scales[:, 1, :])
+            return codes, scales
+
+        def quantise_tokens(rows):
+            codes = quantised.tile([P, GROUP], U32, name="token_codes", align_bytes=64)
+            scales = quantised.tile([P, GROUP], U8, name="token_scales", align_bytes=64)
+            quantise_rows(rows, identity, codes[:], scales[:])
+            return codes, scales
+
+        def project_and_rotate(group, token_operand, weight_operand, factor, out):
+            b, place = divmod(group, GROUPS_PER_BATCH)
+            token_codes, token_scales = token_operand
+            weight_codes, weight_scales = weight_operand
+            rotated = results.tile([P, HEADS, BLOCKS, HEAD_DIM], F32)
+            turned = products.tile([P, HEADS, BLOCKS, HEAD_DIM], F32)
+            for i in range(BLOCKS):
+                block = slice(i * P, (i + 1) * P)
+                straight = sums.tile([P, BANK], F32)
+                swapped = sums.tile([P, BANK], F32)
+                for version, bank in enumerate((straight, swapped)):
+                    nc.tensor.matmul_mx(
+                        out=bank[:],
+                        lhsT=token_codes[:, block].bitcast(FP8X4),
+                        lhsT_scale=token_scales[:, block],
+                        rhs=weight_codes[:, version, :].bitcast(FP8X4),
+                        rhs_scale=weight_scales[:, version, :],
+                        start=True,
+                        stop=True,
+                    )
+                for bank, table, product in (
+                    (straight, cos_table, rotated),
+                    (swapped, sin_signed, turned),
+                ):
+                    nc.vector.scalar_tensor_tensor(
+                        out=product[:, :, i, :],
+                        in0=bank[:].rearrange("p (h d) -> p h d", h=HEADS),
+                        scalar=factor,
+                        in1=table[:, place, i, :].unsqueeze(1).to_broadcast([P, HEADS, HEAD_DIM]),
+                        op0=MULT,
+                        op1=MULT,
+                    )
+                if i % 2 == 1:
+                    two_blocks = slice(i - 1, i + 1)
+                    nc.gpsimd.tensor_tensor(
+                        out=rotated[:, :, two_blocks, :],
+                        in0=rotated[:, :, two_blocks, :],
+                        in1=turned[:, :, two_blocks, :],
+                        op=ADD,
+                    )
+            nc.sync.dma_start(
+                out=out[b, :, place * GROUP : (place + 1) * GROUP, :].rearrange(
+                    "h (p i) d -> p h (i d)", i=BLOCKS
+                ),
+                in_=rotated[:].rearrange("p h i d -> p h (i d)"),
+            )
+
+        def negate_even_features(place):
+            even = sin_signed[:, place].rearrange("p i (j two) -> p (i j) two", two=2)[:, :, 0:1]
+            nc.vector.tensor_scalar_mul(out=even, in0=even, scalar1=-1.0)
+
+        wq_operand = quantise_weight(wq_rows, "wq")
+        token_operand = quantise_tokens(token_rows[0])
+        for group in range(GROUPS):
+            if group < GROUPS_PER_BATCH:
+                negate_even_features(group)
+            project_and_rotate(group, token_operand, wq_operand, 1.0, out_0)
+            if group == 0:
+                wk_operand = quantise_weight(wk_rows, "wk")
+            if group + 1 < GROUPS:
+                next_operand = quantise_tokens(token_rows[group + 1])
+            project_and_rotate(group, token_operand, wk_operand, K_FACTOR, out_1)
+            token_operand = next_operand

@@ -13,13 +13,17 @@ P = 128
 BATCH, SEQ, EMBED, HEADS = 2, 2048, 512, 4
 HEAD_DIM = EMBED // HEADS
 K_FACTOR = HEAD_DIM**-0.5
-BLOCKS = 4
-GROUP = BLOCKS * P
-GROUPS_PER_BATCH = SEQ // GROUP
-GROUPS = BATCH * GROUPS_PER_BATCH
+PACK = 4
 WORDS = EMBED // 2
 BANK = 512
-PACK = 4
+BANK_BLOCKS = BANK // WORDS
+CHUNK_BLOCKS = 4
+CHUNK = CHUNK_BLOCKS * P
+CHUNKS_PER_BATCH = SEQ // CHUNK
+CHUNKS = BATCH * CHUNKS_PER_BATCH
+PIECE_BLOCKS = 2
+PIECES = CHUNK_BLOCKS // PIECE_BLOCKS
+VECTOR_ADDITIONS = 1
 
 FLOPS = 2 * BATCH * SEQ * EMBED * 2 * EMBED
 
@@ -30,11 +34,11 @@ def tile_nucleusxmultiscaleretention_pa_t_kernel(
     nc = tc.nc
     with (
         tc.tile_pool(name="keep", bufs=1) as keep,
-        tc.tile_pool(name="tokens", bufs=GROUPS) as tokens,
-        tc.tile_pool(name="regroup", bufs=3) as regroup,
+        tc.tile_pool(name="tokens", bufs=CHUNKS) as tokens,
+        tc.tile_pool(name="regroup", bufs=2) as regroup,
         tc.tile_pool(name="quantised", bufs=2) as quantised,
-        tc.tile_pool(name="results", bufs=3) as results,
-        tc.tile_pool(name="products", bufs=2) as products,
+        tc.tile_pool(name="results", bufs=6) as results,
+        tc.tile_pool(name="products", bufs=4) as products,
         tc.psum_pool(name="flipped", bufs=2) as flipped,
         tc.psum_pool(name="sums", bufs=3) as sums,
     ):
@@ -47,91 +51,98 @@ def tile_nucleusxmultiscaleretention_pa_t_kernel(
         nc.vector.tensor_copy(out=pair_swap_pairs[:, :, 1:2], in_=identity_pairs[:, :, 0:1])
 
         def load_weight(w, tag):
-            rows = keep.tile([P, BLOCKS * EMBED], BF16, name=tag + "_rows")
+            rows = keep.tile([P, HEADS * EMBED], BF16, name=tag + "_rows")
             nc.sync.dma_start(
-                out=rows[:].rearrange("p (h k) -> p h k", h=BLOCKS),
+                out=rows[:].rearrange("p (h k) -> p h k", h=HEADS),
                 in_=w.rearrange("(h p) k -> p h k", p=P),
             )
             return rows
 
-        def load_tokens(group):
-            b, place = divmod(group, GROUPS_PER_BATCH)
-            rows = tokens.tile([P, BLOCKS * EMBED], BF16, name="token_rows")
+        def load_tokens(chunk):
+            b, place = divmod(chunk, CHUNKS_PER_BATCH)
+            rows = tokens.tile([P, CHUNK_BLOCKS * EMBED], BF16, name="token_rows")
             nc.sync.dma_start(
                 out=rows[:],
-                in_=hidden_states[b, place * GROUP : (place + 1) * GROUP, :].rearrange(
-                    "(p i) k -> p (i k)", i=BLOCKS
+                in_=hidden_states[b, place * CHUNK : (place + 1) * CHUNK, :].rearrange(
+                    "(p i) k -> p (i k)", i=CHUNK_BLOCKS
                 ),
             )
             return rows
 
         def load_table(table, tag):
-            rows = keep.tile([P, GROUPS_PER_BATCH, BLOCKS, HEAD_DIM], BF16, name=tag)
+            rows = keep.tile([P, CHUNKS_PER_BATCH, CHUNK_BLOCKS, HEAD_DIM], BF16, name=tag)
             nc.sync.dma_start(
-                out=rows[:].rearrange("p g i d -> p g (i d)"),
-                in_=table.rearrange("(g p i) d -> p g (i d)", p=P, i=BLOCKS),
+                out=rows[:].rearrange("p c i d -> p c (i d)"),
+                in_=table.rearrange("(c p i) d -> p c (i d)", p=P, i=CHUNK_BLOCKS),
             )
             return rows
 
         wq_rows = load_weight(wq, "wq")
         token_rows = [load_tokens(0)]
-        sin_signed = load_table(sin, "sin_signed")
         cos_table = load_table(cos, "cos_table")
+        sin_signed = load_table(sin, "sin_signed")
         wk_rows = load_weight(wk, "wk")
-        for group in range(1, GROUPS):
-            token_rows.append(load_tokens(group))
+        for chunk in range(1, CHUNKS):
+            token_rows.append(load_tokens(chunk))
 
-        def quantise_rows(rows, permutation, codes, scales):
+        def regroup_rows(rows, permutation, grouped_words, vector_helps):
             words = rows[:].bitcast(F32)
-            grouped = regroup.tile([P, GROUP * PACK], BF16, align_bytes=64)
-            grouped_words = grouped[:].bitcast(F32).rearrange(
-                "p (j r u) -> p j r u", j=BLOCKS, u=2
-            )
-            for first in range(0, BLOCKS, 2):
+            for first in range(0, rows.shape[1] // EMBED, BANK_BLOCKS):
                 bank = flipped.tile([P, BANK], F32)
-                for j in range(2):
+                for j in range(BANK_BLOCKS):
                     for u in range(2):
                         nc.tensor.transpose(
                             bank[:, (2 * j + u) * P : (2 * j + u + 1) * P],
                             words[:, (first + j) * WORDS + u * P : (first + j) * WORDS + (u + 1) * P],
                             permutation[:],
                         )
-                nc.scalar.copy(
-                    out=grouped_words[:, first : first + 2],
-                    in_=bank[:].rearrange("p (j u r) -> p j r u", j=2, u=2),
-                )
-            nc.vector.quantize_mx(out=codes.bitcast(FP8X4), scales=scales, in_=grouped[:])
+                dense = grouped_words[:, first : first + BANK_BLOCKS]
+                hopping = bank[:].rearrange("p (j u r) -> p j r u", j=BANK_BLOCKS, u=2)
+                if vector_helps and first % (2 * BANK_BLOCKS) > 0:
+                    nc.vector.tensor_copy(out=dense, in_=hopping)
+                else:
+                    nc.scalar.copy(out=dense, in_=hopping)
 
-        def quantise_weight(rows, tag):
-            codes = keep.tile([P, 2, GROUP], U32, name=tag + "_codes", align_bytes=64)
-            scales = keep.tile([P, 2, GROUP], U8, name=tag + "_scales", align_bytes=64)
-            quantise_rows(rows, identity, codes[:, 0, :], scales[:, 0, :])
-            quantise_rows(rows, pair_swap, codes[:, 1, :], scales[:, 1, :])
+        def as_words(grouped):
+            return grouped[:].bitcast(F32).rearrange("p (j r u) -> p j r u", r=P, u=2)
+
+        def regroup_weight(rows):
+            grouped_weight = regroup.tile([P, 2 * EMBED * PACK], BF16, align_bytes=64)
+            regroup_rows(rows, identity, as_words(grouped_weight)[:, 0:HEADS], True)
+            regroup_rows(rows, pair_swap, as_words(grouped_weight)[:, HEADS : 2 * HEADS], True)
+            return grouped_weight
+
+        def regroup_tokens(rows, vector_helps):
+            grouped_tokens = regroup.tile([P, CHUNK * PACK], BF16, align_bytes=64)
+            regroup_rows(rows, identity, as_words(grouped_tokens), vector_helps)
+            return grouped_tokens
+
+        def quantise(grouped, pool, tag):
+            columns = grouped.shape[1] // PACK
+            codes = pool.tile([P, columns], U32, name=tag + "_codes", align_bytes=64)
+            scales = pool.tile([P, columns], U8, name=tag + "_scales", align_bytes=64)
+            nc.vector.quantize_mx(out=codes[:].bitcast(FP8X4), scales=scales[:], in_=grouped[:])
             return codes, scales
 
-        def quantise_tokens(rows):
-            codes = quantised.tile([P, GROUP], U32, name="token_codes", align_bytes=64)
-            scales = quantised.tile([P, GROUP], U8, name="token_scales", align_bytes=64)
-            quantise_rows(rows, identity, codes[:], scales[:])
-            return codes, scales
-
-        def project_and_rotate(group, token_operand, weight_operand, factor, out):
-            b, place = divmod(group, GROUPS_PER_BATCH)
+        def project_and_rotate(chunk, piece, token_operand, weight_operand, factor, out, adder):
+            b, place = divmod(chunk, CHUNKS_PER_BATCH)
             token_codes, token_scales = token_operand
             weight_codes, weight_scales = weight_operand
-            rotated = results.tile([P, HEADS, BLOCKS, HEAD_DIM], F32)
-            turned = products.tile([P, HEADS, BLOCKS, HEAD_DIM], F32)
-            for i in range(BLOCKS):
+            rotated = results.tile([P, HEADS, PIECE_BLOCKS, HEAD_DIM], F32)
+            turned = products.tile([P, HEADS, PIECE_BLOCKS, HEAD_DIM], F32)
+            for j in range(PIECE_BLOCKS):
+                i = piece * PIECE_BLOCKS + j
                 block = slice(i * P, (i + 1) * P)
                 straight = sums.tile([P, BANK], F32)
                 swapped = sums.tile([P, BANK], F32)
                 for version, bank in enumerate((straight, swapped)):
+                    features = slice(version * EMBED, (version + 1) * EMBED)
                     nc.tensor.matmul_mx(
                         out=bank[:],
                         lhsT=token_codes[:, block].bitcast(FP8X4),
                         lhsT_scale=token_scales[:, block],
-                        rhs=weight_codes[:, version, :].bitcast(FP8X4),
-                        rhs_scale=weight_scales[:, version, :],
+                        rhs=weight_codes[:, features].bitcast(FP8X4),
+                        rhs_scale=weight_scales[:, features],
                         start=True,
                         stop=True,
                     )
@@ -140,41 +151,59 @@ def tile_nucleusxmultiscaleretention_pa_t_kernel(
                     (swapped, sin_signed, turned),
                 ):
                     nc.vector.scalar_tensor_tensor(
-                        out=product[:, :, i, :],
+                        out=product[:, :, j, :],
                         in0=bank[:].rearrange("p (h d) -> p h d", h=HEADS),
                         scalar=factor,
                         in1=table[:, place, i, :].unsqueeze(1).to_broadcast([P, HEADS, HEAD_DIM]),
                         op0=MULT,
                         op1=MULT,
                     )
-                if i % 2 == 1:
-                    two_blocks = slice(i - 1, i + 1)
-                    nc.gpsimd.tensor_tensor(
-                        out=rotated[:, :, two_blocks, :],
-                        in0=rotated[:, :, two_blocks, :],
-                        in1=turned[:, :, two_blocks, :],
-                        op=ADD,
-                    )
+            adder.tensor_tensor(out=rotated[:], in0=rotated[:], in1=turned[:], op=ADD)
+            out_rows = out[b, :, place * CHUNK : (place + 1) * CHUNK, :].rearrange(
+                "h (p i) d -> p h i d", i=CHUNK_BLOCKS
+            )
+            blocks = slice(piece * PIECE_BLOCKS, (piece + 1) * PIECE_BLOCKS)
             nc.sync.dma_start(
-                out=out[b, :, place * GROUP : (place + 1) * GROUP, :].rearrange(
-                    "h (p i) d -> p h (i d)", i=BLOCKS
-                ),
+                out=out_rows[:, :, blocks, :].rearrange("p h i d -> p h (i d)"),
                 in_=rotated[:].rearrange("p h i d -> p h (i d)"),
             )
 
         def negate_even_features(place):
             even = sin_signed[:, place].rearrange("p i (j two) -> p (i j) two", two=2)[:, :, 0:1]
-            nc.vector.tensor_scalar_mul(out=even, in0=even, scalar1=-1.0)
+            nc.scalar.mul(out=even, in_=even, mul=-1.0)
 
-        wq_operand = quantise_weight(wq_rows, "wq")
-        token_operand = quantise_tokens(token_rows[0])
-        for group in range(GROUPS):
-            if group < GROUPS_PER_BATCH:
-                negate_even_features(group)
-            project_and_rotate(group, token_operand, wq_operand, 1.0, out_0)
-            if group == 0:
-                wk_operand = quantise_weight(wk_rows, "wk")
-            if group + 1 < GROUPS:
-                next_operand = quantise_tokens(token_rows[group + 1])
-            project_and_rotate(group, token_operand, wk_operand, K_FACTOR, out_1)
-            token_operand = next_operand
+        def adder_of(chunk, step):
+            additions_left = (CHUNKS - chunk) * 2 * PIECES - step
+            return nc.vector if additions_left <= VECTOR_ADDITIONS else nc.gpsimd
+
+        with tc.manual_schedule():
+            wq_operand = quantise(regroup_weight(wq_rows), keep, "wq")
+            token_operand = quantise(regroup_tokens(token_rows[0], True), quantised, "token")
+            for chunk in range(CHUNKS):
+                first_chunk = chunk == 0
+                last_chunk = chunk == CHUNKS - 1
+                if chunk < CHUNKS_PER_BATCH:
+                    negate_even_features(chunk)
+                for piece in range(PIECES):
+                    project_and_rotate(
+                        chunk, piece, token_operand, wq_operand, 1.0, out_0, adder_of(chunk, piece)
+                    )
+                    if first_chunk and piece == 0:
+                        wk_grouped = regroup_weight(wk_rows)
+                    if first_chunk and piece == PIECES - 1:
+                        wk_operand = quantise(wk_grouped, keep, "wk")
+                    if not last_chunk and piece == PIECES - 1:
+                        next_grouped = regroup_tokens(token_rows[chunk + 1], False)
+                for piece in range(PIECES):
+                    project_and_rotate(
+                        chunk,
+                        piece,
+                        token_operand,
+                        wk_operand,
+                        K_FACTOR,
+                        out_1,
+                        adder_of(chunk, PIECES + piece),
+                    )
+                    if not last_chunk and piece == 0:
+                        next_operand = quantise(next_grouped, quantised, "token")
+                token_operand = next_operand

@@ -17,13 +17,19 @@ PACK = 4
 WORDS = EMBED // 2
 BANK = 512
 BANK_BLOCKS = BANK // WORDS
-CHUNK_BLOCKS = 4
+QUANTISE_WIDTH = 4096
+CHUNK_BLOCKS = QUANTISE_WIDTH // (P * PACK)
 CHUNK = CHUNK_BLOCKS * P
 CHUNKS_PER_BATCH = SEQ // CHUNK
 CHUNKS = BATCH * CHUNKS_PER_BATCH
 PIECE_BLOCKS = 2
 PIECES = CHUNK_BLOCKS // PIECE_BLOCKS
-VECTOR_ADDITIONS = 1
+ALL_HEADS = (0, HEADS)
+WHOLE = (0, CHUNK_BLOCKS)
+FIRST_HALF = (0, CHUNK_BLOCKS // 2)
+SECOND_HALF = (CHUNK_BLOCKS // 2, CHUNK_BLOCKS)
+REGROUP_AFTER = 0
+QUANTISE_AFTER = 2
 
 FLOPS = 2 * BATCH * SEQ * EMBED * 2 * EMBED
 
@@ -85,9 +91,9 @@ def tile_nucleusxmultiscaleretention_pa_t_kernel(
         for chunk in range(1, CHUNKS):
             token_rows.append(load_tokens(chunk))
 
-        def regroup_rows(rows, permutation, grouped_words, vector_helps):
+        def regroup_rows(rows, blocks, permutation, grouped_words, vector_helps):
             words = rows[:].bitcast(F32)
-            for first in range(0, rows.shape[1] // EMBED, BANK_BLOCKS):
+            for first in range(blocks[0], blocks[1], BANK_BLOCKS):
                 bank = flipped.tile([P, BANK], F32)
                 for j in range(BANK_BLOCKS):
                     for u in range(2):
@@ -106,28 +112,33 @@ def tile_nucleusxmultiscaleretention_pa_t_kernel(
         def as_words(grouped):
             return grouped[:].bitcast(F32).rearrange("p (j r u) -> p j r u", r=P, u=2)
 
-        def regroup_weight(rows):
-            grouped_weight = regroup.tile([P, 2 * EMBED * PACK], BF16, align_bytes=64)
-            regroup_rows(rows, identity, as_words(grouped_weight)[:, 0:HEADS], True)
-            regroup_rows(rows, pair_swap, as_words(grouped_weight)[:, HEADS : 2 * HEADS], True)
-            return grouped_weight
+        def new_operand(pool, tag):
+            grouped = regroup.tile([P, QUANTISE_WIDTH], BF16, align_bytes=64)
+            codes = pool.tile([P, QUANTISE_WIDTH // PACK], U32, name=tag + "_codes", align_bytes=64)
+            scales = pool.tile([P, QUANTISE_WIDTH // PACK], U8, name=tag + "_scales", align_bytes=64)
+            return grouped, codes, scales
 
-        def regroup_tokens(rows, vector_helps):
-            grouped_tokens = regroup.tile([P, CHUNK * PACK], BF16, align_bytes=64)
-            regroup_rows(rows, identity, as_words(grouped_tokens), vector_helps)
-            return grouped_tokens
+        def regroup_weight(rows, operand):
+            words = as_words(operand[0])
+            regroup_rows(rows, ALL_HEADS, identity, words[:, 0:HEADS], True)
+            regroup_rows(rows, ALL_HEADS, pair_swap, words[:, HEADS : 2 * HEADS], True)
 
-        def quantise(grouped, pool, tag):
-            columns = grouped.shape[1] // PACK
-            codes = pool.tile([P, columns], U32, name=tag + "_codes", align_bytes=64)
-            scales = pool.tile([P, columns], U8, name=tag + "_scales", align_bytes=64)
-            nc.vector.quantize_mx(out=codes[:].bitcast(FP8X4), scales=scales[:], in_=grouped[:])
-            return codes, scales
+        def regroup_tokens(rows, blocks, operand):
+            regroup_rows(rows, blocks, identity, as_words(operand[0]), False)
+
+        def quantise(operand, blocks):
+            grouped, codes, scales = operand
+            columns = slice(blocks[0] * P, blocks[1] * P)
+            nc.vector.quantize_mx(
+                out=codes[:, columns].bitcast(FP8X4),
+                scales=scales[:, columns],
+                in_=grouped[:, blocks[0] * P * PACK : blocks[1] * P * PACK],
+            )
 
         def project_and_rotate(chunk, piece, token_operand, weight_operand, factor, out, adder):
             b, place = divmod(chunk, CHUNKS_PER_BATCH)
-            token_codes, token_scales = token_operand
-            weight_codes, weight_scales = weight_operand
+            token_codes, token_scales = token_operand[1:]
+            weight_codes, weight_scales = weight_operand[1:]
             rotated = results.tile([P, HEADS, PIECE_BLOCKS, HEAD_DIM], F32)
             turned = products.tile([P, HEADS, PIECE_BLOCKS, HEAD_DIM], F32)
             for j in range(PIECE_BLOCKS):
@@ -172,13 +183,14 @@ def tile_nucleusxmultiscaleretention_pa_t_kernel(
             even = sin_signed[:, place].rearrange("p i (j two) -> p (i j) two", two=2)[:, :, 0:1]
             nc.scalar.mul(out=even, in_=even, mul=-1.0)
 
-        def adder_of(chunk, step):
-            additions_left = (CHUNKS - chunk) * 2 * PIECES - step
-            return nc.vector if additions_left <= VECTOR_ADDITIONS else nc.gpsimd
-
         with tc.manual_schedule():
-            wq_operand = quantise(regroup_weight(wq_rows), keep, "wq")
-            token_operand = quantise(regroup_tokens(token_rows[0], True), quantised, "token")
+            wq_operand = new_operand(keep, "wq")
+            regroup_weight(wq_rows, wq_operand)
+            quantise(wq_operand, WHOLE)
+            token_operand = new_operand(quantised, "token")
+            for half in (FIRST_HALF, SECOND_HALF):
+                regroup_tokens(token_rows[0], half, token_operand)
+                quantise(token_operand, half)
             for chunk in range(CHUNKS):
                 first_chunk = chunk == 0
                 last_chunk = chunk == CHUNKS - 1
@@ -186,15 +198,15 @@ def tile_nucleusxmultiscaleretention_pa_t_kernel(
                     negate_even_features(chunk)
                 for piece in range(PIECES):
                     project_and_rotate(
-                        chunk, piece, token_operand, wq_operand, 1.0, out_0, adder_of(chunk, piece)
+                        chunk, piece, token_operand, wq_operand, 1.0, out_0, nc.gpsimd
                     )
-                    if first_chunk and piece == 0:
-                        wk_grouped = regroup_weight(wk_rows)
-                    if first_chunk and piece == PIECES - 1:
-                        wk_operand = quantise(wk_grouped, keep, "wk")
-                    if not last_chunk and piece == PIECES - 1:
-                        next_grouped = regroup_tokens(token_rows[chunk + 1], False)
+                    if first_chunk and piece == REGROUP_AFTER:
+                        wk_operand = new_operand(keep, "wk")
+                        regroup_weight(wk_rows, wk_operand)
+                    if first_chunk and piece == QUANTISE_AFTER:
+                        quantise(wk_operand, WHOLE)
                 for piece in range(PIECES):
+                    last_piece = last_chunk and piece == PIECES - 1
                     project_and_rotate(
                         chunk,
                         piece,
@@ -202,8 +214,11 @@ def tile_nucleusxmultiscaleretention_pa_t_kernel(
                         wk_operand,
                         K_FACTOR,
                         out_1,
-                        adder_of(chunk, PIECES + piece),
+                        nc.vector if last_piece else nc.gpsimd,
                     )
-                    if not last_chunk and piece == 0:
-                        next_operand = quantise(next_grouped, quantised, "token")
+                    if not last_chunk and piece == REGROUP_AFTER:
+                        next_operand = new_operand(quantised, "token")
+                        regroup_tokens(token_rows[chunk + 1], WHOLE, next_operand)
+                    if not last_chunk and piece == QUANTISE_AFTER:
+                        quantise(next_operand, WHOLE)
                 token_operand = next_operand

@@ -16,20 +16,11 @@ K_FACTOR = HEAD_DIM**-0.5
 PACK = 4
 WORDS = EMBED // 2
 BANK = 512
-BANK_BLOCKS = BANK // WORDS
-QUANTISE_WIDTH = 4096
-CHUNK_BLOCKS = QUANTISE_WIDTH // (P * PACK)
-CHUNK = CHUNK_BLOCKS * P
-CHUNKS_PER_BATCH = SEQ // CHUNK
-CHUNKS = BATCH * CHUNKS_PER_BATCH
-PIECE_BLOCKS = 2
-PIECES = CHUNK_BLOCKS // PIECE_BLOCKS
-ALL_HEADS = (0, HEADS)
-WHOLE = (0, CHUNK_BLOCKS)
-FIRST_HALF = (0, CHUNK_BLOCKS // 2)
-SECOND_HALF = (CHUNK_BLOCKS // 2, CHUNK_BLOCKS)
-REGROUP_AFTER = 0
-QUANTISE_AFTER = 2
+BLOCKS = BANK // WORDS
+GROUP = BLOCKS * P
+GROUPS_PER_BATCH = SEQ // GROUP
+GROUPS = BATCH * GROUPS_PER_BATCH
+K_LAG = 2
 
 FLOPS = 2 * BATCH * SEQ * EMBED * 2 * EMBED
 
@@ -40,9 +31,9 @@ def tile_nucleusxmultiscaleretention_pa_t_kernel(
     nc = tc.nc
     with (
         tc.tile_pool(name="keep", bufs=1) as keep,
-        tc.tile_pool(name="tokens", bufs=CHUNKS) as tokens,
-        tc.tile_pool(name="regroup", bufs=2) as regroup,
-        tc.tile_pool(name="quantised", bufs=2) as quantised,
+        tc.tile_pool(name="tokens", bufs=GROUPS) as tokens,
+        tc.tile_pool(name="regroup", bufs=3) as regroup,
+        tc.tile_pool(name="quantised", bufs=K_LAG + 3) as quantised,
         tc.tile_pool(name="results", bufs=6) as results,
         tc.tile_pool(name="products", bufs=4) as products,
         tc.psum_pool(name="flipped", bufs=2) as flipped,
@@ -58,91 +49,87 @@ def tile_nucleusxmultiscaleretention_pa_t_kernel(
 
         def load_weight(w, tag):
             rows = keep.tile([P, HEADS * EMBED], BF16, name=tag + "_rows")
-            nc.sync.dma_start(
-                out=rows[:].rearrange("p (h k) -> p h k", h=HEADS),
-                in_=w.rearrange("(h p) k -> p h k", p=P),
-            )
+            by_head = rows[:].rearrange("p (h k) -> p h k", h=HEADS)
+            w_by_head = w.rearrange("(h p) k -> p h k", p=P)
+            for first in range(0, HEADS, BLOCKS):
+                nc.sync.dma_start(
+                    out=by_head[:, first : first + BLOCKS], in_=w_by_head[:, first : first + BLOCKS]
+                )
             return rows
 
-        def load_tokens(chunk):
-            b, place = divmod(chunk, CHUNKS_PER_BATCH)
-            rows = tokens.tile([P, CHUNK_BLOCKS * EMBED], BF16, name="token_rows")
+        def load_tokens(group):
+            b, place = divmod(group, GROUPS_PER_BATCH)
+            rows = tokens.tile([P, BLOCKS * EMBED], BF16, name="token_rows")
             nc.sync.dma_start(
                 out=rows[:],
-                in_=hidden_states[b, place * CHUNK : (place + 1) * CHUNK, :].rearrange(
-                    "(p i) k -> p (i k)", i=CHUNK_BLOCKS
+                in_=hidden_states[b, place * GROUP : (place + 1) * GROUP, :].rearrange(
+                    "(p i) k -> p (i k)", i=BLOCKS
                 ),
             )
             return rows
 
         def load_table(table, tag):
-            rows = keep.tile([P, CHUNKS_PER_BATCH, CHUNK_BLOCKS, HEAD_DIM], BF16, name=tag)
+            rows = keep.tile([P, GROUPS_PER_BATCH, BLOCKS, HEAD_DIM], BF16, name=tag)
             nc.sync.dma_start(
-                out=rows[:].rearrange("p c i d -> p c (i d)"),
-                in_=table.rearrange("(c p i) d -> p c (i d)", p=P, i=CHUNK_BLOCKS),
+                out=rows[:].rearrange("p g i d -> p g (i d)"),
+                in_=table.rearrange("(g p i) d -> p g (i d)", p=P, i=BLOCKS),
             )
             return rows
 
         wq_rows = load_weight(wq, "wq")
-        token_rows = [load_tokens(0)]
+        token_rows = [load_tokens(0), load_tokens(1)]
         cos_table = load_table(cos, "cos_table")
         sin_signed = load_table(sin, "sin_signed")
         wk_rows = load_weight(wk, "wk")
-        for chunk in range(1, CHUNKS):
-            token_rows.append(load_tokens(chunk))
+        for group in range(2, GROUPS):
+            token_rows.append(load_tokens(group))
 
-        def regroup_rows(rows, blocks, permutation, grouped_words, vector_helps):
+        def regroup_rows(rows, permutation, grouped, vector_helps):
             words = rows[:].bitcast(F32)
-            for first in range(blocks[0], blocks[1], BANK_BLOCKS):
+            grouped_words = grouped.bitcast(F32).rearrange("p (j r u) -> p j r u", r=P, u=2)
+            for first in range(0, rows.shape[1] // EMBED, BLOCKS):
                 bank = flipped.tile([P, BANK], F32)
-                for j in range(BANK_BLOCKS):
+                for j in range(BLOCKS):
                     for u in range(2):
                         nc.tensor.transpose(
                             bank[:, (2 * j + u) * P : (2 * j + u + 1) * P],
                             words[:, (first + j) * WORDS + u * P : (first + j) * WORDS + (u + 1) * P],
                             permutation[:],
                         )
-                dense = grouped_words[:, first : first + BANK_BLOCKS]
-                hopping = bank[:].rearrange("p (j u r) -> p j r u", j=BANK_BLOCKS, u=2)
-                if vector_helps and first % (2 * BANK_BLOCKS) > 0:
+                dense = grouped_words[:, first : first + BLOCKS]
+                hopping = bank[:].rearrange("p (j u r) -> p j r u", j=BLOCKS, u=2)
+                if vector_helps and first > 0:
                     nc.vector.tensor_copy(out=dense, in_=hopping)
                 else:
                     nc.scalar.copy(out=dense, in_=hopping)
 
-        def as_words(grouped):
-            return grouped[:].bitcast(F32).rearrange("p (j r u) -> p j r u", r=P, u=2)
+        def regroup_weight(rows, vector_helps):
+            grouped_weight = keep.tile([P, 2 * EMBED * PACK], BF16, align_bytes=64)
+            straight_half = grouped_weight[:, 0 : EMBED * PACK]
+            swapped_half = grouped_weight[:, EMBED * PACK : 2 * EMBED * PACK]
+            regroup_rows(rows, identity, straight_half, vector_helps)
+            regroup_rows(rows, pair_swap, swapped_half, vector_helps)
+            return grouped_weight
 
-        def new_operand(pool, tag):
-            grouped = regroup.tile([P, QUANTISE_WIDTH], BF16, align_bytes=64)
-            codes = pool.tile([P, QUANTISE_WIDTH // PACK], U32, name=tag + "_codes", align_bytes=64)
-            scales = pool.tile([P, QUANTISE_WIDTH // PACK], U8, name=tag + "_scales", align_bytes=64)
-            return grouped, codes, scales
+        def regroup_tokens(group):
+            grouped_tokens = regroup.tile([P, GROUP * PACK], BF16, align_bytes=64)
+            regroup_rows(token_rows[group], identity, grouped_tokens[:], False)
+            return grouped_tokens
 
-        def regroup_weight(rows, operand):
-            words = as_words(operand[0])
-            regroup_rows(rows, ALL_HEADS, identity, words[:, 0:HEADS], True)
-            regroup_rows(rows, ALL_HEADS, pair_swap, words[:, HEADS : 2 * HEADS], True)
+        def quantise(grouped, pool, tag):
+            columns = grouped.shape[1] // PACK
+            codes = pool.tile([P, columns], U32, name=tag + "_codes", align_bytes=64)
+            scales = pool.tile([P, columns], U8, name=tag + "_scales", align_bytes=64)
+            nc.vector.quantize_mx(out=codes[:].bitcast(FP8X4), scales=scales[:], in_=grouped[:])
+            return codes, scales
 
-        def regroup_tokens(rows, blocks, operand):
-            regroup_rows(rows, blocks, identity, as_words(operand[0]), False)
-
-        def quantise(operand, blocks):
-            grouped, codes, scales = operand
-            columns = slice(blocks[0] * P, blocks[1] * P)
-            nc.vector.quantize_mx(
-                out=codes[:, columns].bitcast(FP8X4),
-                scales=scales[:, columns],
-                in_=grouped[:, blocks[0] * P * PACK : blocks[1] * P * PACK],
-            )
-
-        def project_and_rotate(chunk, piece, token_operand, weight_operand, factor, out, adder):
-            b, place = divmod(chunk, CHUNKS_PER_BATCH)
-            token_codes, token_scales = token_operand[1:]
-            weight_codes, weight_scales = weight_operand[1:]
-            rotated = results.tile([P, HEADS, PIECE_BLOCKS, HEAD_DIM], F32)
-            turned = products.tile([P, HEADS, PIECE_BLOCKS, HEAD_DIM], F32)
-            for j in range(PIECE_BLOCKS):
-                i = piece * PIECE_BLOCKS + j
+        def project_and_rotate(group, token_operand, weight_operand, factor, out, adder):
+            b, place = divmod(group, GROUPS_PER_BATCH)
+            token_codes, token_scales = token_operand
+            weight_codes, weight_scales = weight_operand
+            rotated = results.tile([P, HEADS, BLOCKS, HEAD_DIM], F32)
+            turned = products.tile([P, HEADS, BLOCKS, HEAD_DIM], F32)
+            for i in range(BLOCKS):
                 block = slice(i * P, (i + 1) * P)
                 straight = sums.tile([P, BANK], F32)
                 swapped = sums.tile([P, BANK], F32)
@@ -162,7 +149,7 @@ def tile_nucleusxmultiscaleretention_pa_t_kernel(
                     (swapped, sin_signed, turned),
                 ):
                     nc.vector.scalar_tensor_tensor(
-                        out=product[:, :, j, :],
+                        out=product[:, :, i, :],
                         in0=bank[:].rearrange("p (h d) -> p h d", h=HEADS),
                         scalar=factor,
                         in1=table[:, place, i, :].unsqueeze(1).to_broadcast([P, HEADS, HEAD_DIM]),
@@ -170,12 +157,10 @@ def tile_nucleusxmultiscaleretention_pa_t_kernel(
                         op1=MULT,
                     )
             adder.tensor_tensor(out=rotated[:], in0=rotated[:], in1=turned[:], op=ADD)
-            out_rows = out[b, :, place * CHUNK : (place + 1) * CHUNK, :].rearrange(
-                "h (p i) d -> p h i d", i=CHUNK_BLOCKS
-            )
-            blocks = slice(piece * PIECE_BLOCKS, (piece + 1) * PIECE_BLOCKS)
             nc.sync.dma_start(
-                out=out_rows[:, :, blocks, :].rearrange("p h i d -> p h (i d)"),
+                out=out[b, :, place * GROUP : (place + 1) * GROUP, :].rearrange(
+                    "h (p i) d -> p h (i d)", i=BLOCKS
+                ),
                 in_=rotated[:].rearrange("p h i d -> p h (i d)"),
             )
 
@@ -184,41 +169,26 @@ def tile_nucleusxmultiscaleretention_pa_t_kernel(
             nc.scalar.mul(out=even, in_=even, mul=-1.0)
 
         with tc.manual_schedule():
-            wq_operand = new_operand(keep, "wq")
-            regroup_weight(wq_rows, wq_operand)
-            quantise(wq_operand, WHOLE)
-            token_operand = new_operand(quantised, "token")
-            for half in (FIRST_HALF, SECOND_HALF):
-                regroup_tokens(token_rows[0], half, token_operand)
-                quantise(token_operand, half)
-            for chunk in range(CHUNKS):
-                first_chunk = chunk == 0
-                last_chunk = chunk == CHUNKS - 1
-                if chunk < CHUNKS_PER_BATCH:
-                    negate_even_features(chunk)
-                for piece in range(PIECES):
+            wq_operand = quantise(regroup_weight(wq_rows, True), keep, "wq")
+            regrouped = {0: regroup_tokens(0)}
+            operand = {0: quantise(regrouped[0], quantised, "token")}
+            regrouped[1] = regroup_tokens(1)
+            negate_even_features(0)
+            for step in range(GROUPS + K_LAG):
+                if step + 1 < GROUPS_PER_BATCH:
+                    negate_even_features(step + 1)
+                if step < GROUPS:
+                    project_and_rotate(step, operand[step], wq_operand, 1.0, out_0, nc.gpsimd)
+                if step == 0:
+                    wk_grouped = regroup_weight(wk_rows, False)
+                if step + 1 < GROUPS:
+                    operand[step + 1] = quantise(regrouped[step + 1], quantised, "token")
+                if step == K_LAG - 1:
+                    wk_operand = quantise(wk_grouped, keep, "wk")
+                if step >= K_LAG:
+                    adder = nc.vector if step == GROUPS + K_LAG - 1 else nc.gpsimd
                     project_and_rotate(
-                        chunk, piece, token_operand, wq_operand, 1.0, out_0, nc.gpsimd
+                        step - K_LAG, operand[step - K_LAG], wk_operand, K_FACTOR, out_1, adder
                     )
-                    if first_chunk and piece == REGROUP_AFTER:
-                        wk_operand = new_operand(keep, "wk")
-                        regroup_weight(wk_rows, wk_operand)
-                    if first_chunk and piece == QUANTISE_AFTER:
-                        quantise(wk_operand, WHOLE)
-                for piece in range(PIECES):
-                    last_piece = last_chunk and piece == PIECES - 1
-                    project_and_rotate(
-                        chunk,
-                        piece,
-                        token_operand,
-                        wk_operand,
-                        K_FACTOR,
-                        out_1,
-                        nc.vector if last_piece else nc.gpsimd,
-                    )
-                    if not last_chunk and piece == REGROUP_AFTER:
-                        next_operand = new_operand(quantised, "token")
-                        regroup_tokens(token_rows[chunk + 1], WHOLE, next_operand)
-                    if not last_chunk and piece == QUANTISE_AFTER:
-                        quantise(next_operand, WHOLE)
-                token_operand = next_operand
+                if step + 2 < GROUPS:
+                    regrouped[step + 2] = regroup_tokens(step + 2)

import concourse.mybir as mybir
from concourse.masks import make_identity

F32 = mybir.dt.float32
BF16 = mybir.dt.bfloat16
U32 = mybir.dt.uint32
U8 = mybir.dt.uint8
FP8X4 = mybir.dt.float8_e4m3fn_x4
MULT = mybir.AluOpType.mult
ADD = mybir.AluOpType.add

P = 128
BATCH, SEQ, EMBED, HEADS = 2, 2048, 512, 4
HEAD_DIM = EMBED // HEADS
K_FACTOR = HEAD_DIM**-0.5
PACK = 4
WORDS = EMBED // 2
BANK = 512
BLOCKS = BANK // WORDS
GROUP = BLOCKS * P
GROUPS_PER_BATCH = SEQ // GROUP
GROUPS = BATCH * GROUPS_PER_BATCH
K_LAG = 2

FLOPS = 2 * BATCH * SEQ * EMBED * 2 * EMBED


def tile_nucleusxmultiscaleretention_pa_t_kernel(
    tc, hidden_states, wq, wk, sin, cos, out_0, out_1
):
    nc = tc.nc
    with (
        tc.tile_pool(name="keep", bufs=1) as keep,
        tc.tile_pool(name="tokens", bufs=GROUPS) as tokens,
        tc.tile_pool(name="regroup", bufs=3) as regroup,
        tc.tile_pool(name="quantised", bufs=K_LAG + 3) as quantised,
        tc.tile_pool(name="results", bufs=6) as results,
        tc.tile_pool(name="products", bufs=4) as products,
        tc.psum_pool(name="flipped", bufs=2) as flipped,
        tc.psum_pool(name="sums", bufs=3) as sums,
    ):
        identity = keep.tile([P, P], F32)
        make_identity(nc, identity[:])
        pair_swap = keep.tile([P, P], F32)
        identity_pairs = identity[:].rearrange("p (j two) -> p j two", two=2)
        pair_swap_pairs = pair_swap[:].rearrange("p (j two) -> p j two", two=2)
        nc.vector.tensor_copy(out=pair_swap_pairs[:, :, 0:1], in_=identity_pairs[:, :, 1:2])
        nc.vector.tensor_copy(out=pair_swap_pairs[:, :, 1:2], in_=identity_pairs[:, :, 0:1])

        def load_weight(w, tag):
            rows = keep.tile([P, HEADS * EMBED], BF16, name=tag + "_rows")
            by_head = rows[:].rearrange("p (h k) -> p h k", h=HEADS)
            w_by_head = w.rearrange("(h p) k -> p h k", p=P)
            for first in range(0, HEADS, BLOCKS):
                nc.sync.dma_start(
                    out=by_head[:, first : first + BLOCKS], in_=w_by_head[:, first : first + BLOCKS]
                )
            return rows

        def load_tokens(group):
            b, place = divmod(group, GROUPS_PER_BATCH)
            rows = tokens.tile([P, BLOCKS * EMBED], BF16, name="token_rows")
            nc.sync.dma_start(
                out=rows[:],
                in_=hidden_states[b, place * GROUP : (place + 1) * GROUP, :].rearrange(
                    "(p i) k -> p (i k)", i=BLOCKS
                ),
            )
            return rows

        def load_table(table, tag):
            rows = keep.tile([P, GROUPS_PER_BATCH, BLOCKS, HEAD_DIM], BF16, name=tag)
            nc.sync.dma_start(
                out=rows[:].rearrange("p g i d -> p g (i d)"),
                in_=table.rearrange("(g p i) d -> p g (i d)", p=P, i=BLOCKS),
            )
            return rows

        wq_rows = load_weight(wq, "wq")
        token_rows = [load_tokens(0), load_tokens(1)]
        cos_table = load_table(cos, "cos_table")
        sin_signed = load_table(sin, "sin_signed")
        wk_rows = load_weight(wk, "wk")
        for group in range(2, GROUPS):
            token_rows.append(load_tokens(group))

        def regroup_rows(rows, permutation, grouped, vector_helps):
            words = rows[:].bitcast(F32)
            grouped_words = grouped.bitcast(F32).rearrange("p (j r u) -> p j r u", r=P, u=2)
            for first in range(0, rows.shape[1] // EMBED, BLOCKS):
                bank = flipped.tile([P, BANK], F32)
                for j in range(BLOCKS):
                    for u in range(2):
                        nc.tensor.transpose(
                            bank[:, (2 * j + u) * P : (2 * j + u + 1) * P],
                            words[:, (first + j) * WORDS + u * P : (first + j) * WORDS + (u + 1) * P],
                            permutation[:],
                        )
                dense = grouped_words[:, first : first + BLOCKS]
                hopping = bank[:].rearrange("p (j u r) -> p j r u", j=BLOCKS, u=2)
                if vector_helps and first > 0:
                    nc.vector.tensor_copy(out=dense, in_=hopping)
                else:
                    nc.scalar.copy(out=dense, in_=hopping)

        def regroup_weight(rows, vector_helps):
            grouped_weight = keep.tile([P, 2 * EMBED * PACK], BF16, align_bytes=64)
            straight_half = grouped_weight[:, 0 : EMBED * PACK]
            swapped_half = grouped_weight[:, EMBED * PACK : 2 * EMBED * PACK]
            regroup_rows(rows, identity, straight_half, vector_helps)
            regroup_rows(rows, pair_swap, swapped_half, vector_helps)
            return grouped_weight

        def regroup_tokens(group):
            grouped_tokens = regroup.tile([P, GROUP * PACK], BF16, align_bytes=64)
            regroup_rows(token_rows[group], identity, grouped_tokens[:], False)
            return grouped_tokens

        def quantise(grouped, pool, tag):
            columns = grouped.shape[1] // PACK
            codes = pool.tile([P, columns], U32, name=tag + "_codes", align_bytes=64)
            scales = pool.tile([P, columns], U8, name=tag + "_scales", align_bytes=64)
            nc.vector.quantize_mx(out=codes[:].bitcast(FP8X4), scales=scales[:], in_=grouped[:])
            return codes, scales

        def project_and_rotate(group, token_operand, weight_operand, factor, out, adder):
            b, place = divmod(group, GROUPS_PER_BATCH)
            token_codes, token_scales = token_operand
            weight_codes, weight_scales = weight_operand
            rotated = results.tile([P, HEADS, BLOCKS, HEAD_DIM], F32)
            turned = products.tile([P, HEADS, BLOCKS, HEAD_DIM], F32)
            for i in range(BLOCKS):
                block = slice(i * P, (i + 1) * P)
                straight = sums.tile([P, BANK], F32)
                swapped = sums.tile([P, BANK], F32)
                for version, bank in enumerate((straight, swapped)):
                    features = slice(version * EMBED, (version + 1) * EMBED)
                    nc.tensor.matmul_mx(
                        out=bank[:],
                        lhsT=token_codes[:, block].bitcast(FP8X4),
                        lhsT_scale=token_scales[:, block],
                        rhs=weight_codes[:, features].bitcast(FP8X4),
                        rhs_scale=weight_scales[:, features],
                        start=True,
                        stop=True,
                    )
                for bank, table, product in (
                    (straight, cos_table, rotated),
                    (swapped, sin_signed, turned),
                ):
                    nc.vector.scalar_tensor_tensor(
                        out=product[:, :, i, :],
                        in0=bank[:].rearrange("p (h d) -> p h d", h=HEADS),
                        scalar=factor,
                        in1=table[:, place, i, :].unsqueeze(1).to_broadcast([P, HEADS, HEAD_DIM]),
                        op0=MULT,
                        op1=MULT,
                    )
            adder.tensor_tensor(out=rotated[:], in0=rotated[:], in1=turned[:], op=ADD)
            nc.sync.dma_start(
                out=out[b, :, place * GROUP : (place + 1) * GROUP, :].rearrange(
                    "h (p i) d -> p h (i d)", i=BLOCKS
                ),
                in_=rotated[:].rearrange("p h i d -> p h (i d)"),
            )

        def negate_even_features(place):
            even = sin_signed[:, place].rearrange("p i (j two) -> p (i j) two", two=2)[:, :, 0:1]
            nc.scalar.mul(out=even, in_=even, mul=-1.0)

        with tc.manual_schedule():
            wq_operand = quantise(regroup_weight(wq_rows, True), keep, "wq")
            regrouped = {0: regroup_tokens(0)}
            operand = {0: quantise(regrouped[0], quantised, "token")}
            regrouped[1] = regroup_tokens(1)
            negate_even_features(0)
            for step in range(GROUPS + K_LAG):
                if step + 1 < GROUPS_PER_BATCH:
                    negate_even_features(step + 1)
                if step < GROUPS:
                    project_and_rotate(step, operand[step], wq_operand, 1.0, out_0, nc.gpsimd)
                if step == 0:
                    wk_grouped = regroup_weight(wk_rows, False)
                if step + 1 < GROUPS:
                    operand[step + 1] = quantise(regrouped[step + 1], quantised, "token")
                if step == K_LAG - 1:
                    wk_operand = quantise(wk_grouped, keep, "wk")
                if step >= K_LAG:
                    adder = nc.vector if step == GROUPS + K_LAG - 1 else nc.gpsimd
                    project_and_rotate(
                        step - K_LAG, operand[step - K_LAG], wk_operand, K_FACTOR, out_1, adder
                    )
                if step + 2 < GROUPS:
                    regrouped[step + 2] = regroup_tokens(step + 2)
